import numpy as np
import ml_dtypes


def mxq(x, axis, fmt="e4m3"):
    dtype, down = {"e4m3": (ml_dtypes.float8_e4m3fn, 7), "e5m2": (ml_dtypes.float8_e5m2, 14)}[fmt]
    v = np.moveaxis(np.asarray(x, np.float32).astype(ml_dtypes.bfloat16).astype(np.float64), axis, -1)
    blocks = v.reshape(v.shape[:-1] + (-1, 32))
    amax = np.abs(blocks).max(-1, keepdims=True)
    byte = np.maximum(np.where(amax > 0, np.frexp(amax)[1] - 1 + 127, 0) - down, 1)
    scale = np.exp2(byte - 127.0)
    codes = (blocks / scale).astype(np.float32).astype(dtype).astype(np.float64)
    return np.moveaxis((codes * scale).reshape(v.shape), -1, axis)


WIDE = False


def mx_kscale(k):
    if not WIDE:
        return np.ones(k)
    levels = np.array([10, -10, 5, -5, 0])
    if k % 512:
        return np.exp2(np.random.permutation(np.resize(levels, k // 32))).repeat(32)
    a = np.empty((k // 512, 16))
    for p in range(k // 512):
        a[p, :8] = np.random.permutation(np.resize(levels, 8))
        for g in range(8):
            far = levels[np.abs(levels - a[p, g]) >= 10]
            a[p, g + 8] = far[np.random.randint(len(far))]
    return np.exp2(a.ravel()).repeat(32)


BF16 = ml_dtypes.bfloat16


def bf(x):
    return np.asarray(x, np.float32).astype(BF16)


def f64(x):
    return np.asarray(x).astype(np.float64)


B, N, D, F1, F2, F3, G1, G2 = 8, 32, 2048, 2048, 4096, 2048, 2048, 2048
ALPHA = 0.2


def lrelu(v):
    return np.maximum(v, ALPHA * v)


def setup_inputs():
    s, t = mx_kscale(D), mx_kscale(F1)
    ss = np.concatenate([s, s])
    return {"x": bf(np.random.standard_normal((B, N, D)) * s),
            "fe_w0": bf(np.random.standard_normal((D + D, F1)) / np.sqrt(D + D) / ss[:, None] * t),
            "fe_b0": bf(np.random.standard_normal(F1) * 0.3 * t),
            "fe_w1": bf(np.random.standard_normal((F1, F2)) * 1.4 / np.sqrt(F1) / t[:, None]),
            "fe_b1": bf(np.random.standard_normal(F2) * 0.3)}


def reference(x, fe_w0, fe_b0, fe_w1, fe_b1):
    xq = mxq(f64(x), 2, "e4m3")
    w0 = f64(fe_w0)
    u = xq @ mxq(w0[:D], 0, "e4m3")
    v = xq @ mxq(w0[D:], 0, "e4m3")
    e1 = lrelu(u[:, :, None, :] + v[:, None, :, :] + f64(fe_b0))
    return lrelu((mxq(e1, 3, "e4m3") @ mxq(f64(fe_w1), 0, "e4m3")) + f64(fe_b1))

@@ -1,0 +1,307 @@
+from contextlib import ExitStack
+
+import concourse.mybir as mybir
+from concourse.masks import make_identity
+
+FLOPS = 2 * 256 * 2048 * 4096 + 2 * 8192 * 2048 * 4096
+
+F32 = mybir.dt.float32
+BF16 = mybir.dt.bfloat16
+U32 = mybir.dt.uint32
+U8 = mybir.dt.uint8
+FP8X4 = mybir.dt.float8_e4m3fn_x4
+ACT = mybir.ActivationFunctionType
+ALU = mybir.AluOpType
+
+P = 128
+NODES = 32
+TOK = 256
+D = 2048
+F1 = 2048
+F2 = 4096
+ALPHA = 0.2
+N_CHUNKS = 64
+N_CYCLES = 64
+LEAD = 5
+
+
+def tile_graph_gan_pa_l_kernel(tc, x, fe_w0, fe_b0, fe_w1, fe_b1, out):
+    nc = tc.nc
+    x2 = x.rearrange("b n d -> (b n) d")
+    out2 = out.rearrange("b i j c -> (b i j) c")
+
+    with ExitStack() as ctx:
+        const = ctx.enter_context(tc.tile_pool(name="const", bufs=1))
+        keep = ctx.enter_context(tc.tile_pool(name="keep", bufs=1))
+        stream = ctx.enter_context(tc.tile_pool(name="stream", bufs=3))
+        psum = ctx.enter_context(tc.psum_pool(name="psum", bufs=8))
+
+        ident = const.tile([P, P], F32, name="ident")
+        make_identity(nc, ident[:])
+        warm = const.tile([P, 8], F32, name="warm")
+        nc.vector.memset(warm[:], 0.0)
+        warm2 = const.tile([P, 8], F32, name="warm2")
+        nc.scalar.activation(out=warm2[:], in_=warm[:], func=ACT.Identity)
+        b0raw = const.tile([P, 4, 4], BF16, name="b0raw")
+        b0f = const.tile([P, 16], F32, name="b0f")
+        b1t = const.tile([P, F2], BF16, name="b1t")
+
+        w1c = keep.tile([P, 4, F2], U32, name="w1c", align_bytes=64)
+        w1s = keep.tile([P, F2], U8, name="w1s", align_bytes=64)
+        u_sb = keep.tile([P, 16, TOK], F32, name="u_sb")
+        v_sb = keep.tile([P, 16, TOK], F32, name="v_sb")
+
+        def load_chunk(rows):
+            raw = stream.tile([P, 4, 1024], BF16, name="raw", tag="raw", bufs=3)
+            nc.sync.dma_start(out=raw[:], in_=rows.rearrange("(p j) f -> p j f", j=4))
+            return raw
+
+        def new_grp():
+            grp = stream.tile([P, 2048], BF16, name="grp", tag="grp", bufs=4, align_bytes=64)
+            return grp
+
+        def copy_on(which, dst, src):
+            if which == 0:
+                nc.vector.tensor_copy(out=dst, in_=src)
+            else:
+                nc.scalar.copy(out=dst, in_=src)
+
+        with tc.tile_pool(name="head", bufs=1) as head:
+            xc = head.tile([P, 4 * TOK], U32, name="xc", align_bytes=64)
+            xs = head.tile([P, 4 * TOK], U8, name="xs", align_bytes=64)
+            w0c = []
+            w0s = []
+            for h in range(2):
+                w0c_h = head.tile([P, 4, F1], U32, name="w0c%d" % h, align_bytes=64)
+                w0s_h = head.tile([P, F1], U8, name="w0s%d" % h, align_bytes=64)
+                w0c.append(w0c_h)
+                w0s.append(w0s_h)
+
+            xraw = []
+            for tt in range(2):
+                xr = new_grp()
+                nc.sync.dma_start(out=xr[:], in_=x2[P * tt : P * (tt + 1), :])
+                xraw.append(xr)
+            nc.sync.dma_start(out=b0raw[:], in_=fe_b0.rearrange("(g p t) -> p g t", g=4, t=4))
+            nc.vector.tensor_copy(out=b0f[:], in_=b0raw[:].rearrange("p g t -> p (g t)"))
+
+            for gh in range(2):
+                xg = new_grp()
+                for gl in range(2):
+                    g = 2 * gh + gl
+                    pt = psum.tile([P, 512], F32, name="pt", tag="ps")
+                    for tt in range(2):
+                        words = xraw[tt][:].bitcast(F32)
+                        for u in range(2):
+                            col = (2 * tt + u) * P
+                            nc.tensor.transpose(
+                                pt[:, col : col + P],
+                                words[:, 256 * g + u : 256 * (g + 1) : 2],
+                                ident[:],
+                            )
+                    nc.vector.tensor_copy(
+                        out=xg[:, 1024 * gl : 1024 * (gl + 1)]
+                        .bitcast(F32)
+                        .rearrange("p (tt r u) -> p tt r u", tt=2, u=2),
+                        in_=pt[:].rearrange("p (tt u r) -> p tt r u", tt=2, u=2),
+                    )
+                nc.vector.quantize_mx(
+                    out=xc[:, 512 * gh : 512 * (gh + 1)].bitcast(FP8X4),
+                    scales=xs[:, 512 * gh : 512 * (gh + 1)],
+                    in_=xg[:],
+                )
+
+            for h in range(2):
+                for gk in range(4):
+                    for fh in range(2):
+                        r0 = 2048 * h + 512 * gk
+                        raw = load_chunk(fe_w0[r0 : r0 + 512, 1024 * fh : 1024 * (fh + 1)])
+                        for gl in range(2):
+                            gf = 2 * fh + gl
+                            grp = new_grp()
+                            copy_on(
+                                gl,
+                                grp[:].rearrange("p (t m j) -> p t m j", t=4, j=4),
+                                raw[:, :, 512 * gl : 512 * (gl + 1)].rearrange("p j (m t) -> p t m j", t=4),
+                            )
+                            nc.vector.quantize_mx(
+                                out=w0c[h][:, gk, 512 * gf : 512 * (gf + 1)].bitcast(FP8X4),
+                                scales=w0s[h][4 * gk : P, 512 * gf : 512 * (gf + 1)],
+                                in_=grp[:],
+                            )
+                for gf in range(4):
+                    for th in range(2):
+                        ps1 = psum.tile([P, 512], F32, name="ps1", tag="ps")
+                        for tl in range(2):
+                            t = 2 * th + tl
+                            c0 = 512 * gf + P * t
+                            for gk in range(4):
+                                nc.tensor.matmul_mx(
+                                    out=ps1[:, TOK * tl : TOK * (tl + 1)],
+                                    lhsT=w0c[h][:, gk, c0 : c0 + P].bitcast(FP8X4),
+                                    lhsT_scale=w0s[h][4 * gk : P, c0 : c0 + P],
+                                    rhs=xc[:, TOK * gk : TOK * (gk + 1)].bitcast(FP8X4),
+                                    rhs_scale=xs[:, TOK * gk : TOK * (gk + 1)],
+                                    start=(gk == 0),
+                                    stop=(gk == 3),
+                                )
+                        gt = 4 * gf + 2 * th
+                        if h == 0:
+                            dst = u_sb[:, gt : gt + 2, :].rearrange("p a r -> p (a r)")
+                            if th == 0:
+                                nc.vector.tensor_scalar_mul(out=dst, in0=ps1[:], scalar1=ALPHA)
+                            else:
+                                nc.scalar.activation(out=dst, in_=ps1[:], func=ACT.Copy, scale=ALPHA)
+                        else:
+                            for tl in range(2):
+                                src = ps1[:, TOK * tl : TOK * (tl + 1)]
+                                bias = b0f[:, gt + tl : gt + tl + 1]
+                                if th == 0:
+                                    nc.vector.tensor_scalar_add(out=v_sb[:, gt + tl, :], in0=src, scalar1=bias)
+                                else:
+                                    nc.scalar.activation(
+                                        out=v_sb[:, gt + tl, :], in_=src, func=ACT.Identity, bias=bias, scale=1.0
+                                    )
+
+        work = ctx.enter_context(tc.tile_pool(name="work", bufs=2))
+
+        def w1_quarter(nh):
+            for g in range(4):
+                raw = load_chunk(fe_w1[512 * g : 512 * (g + 1), 1024 * nh : 1024 * (nh + 1)])
+                for nl in range(2):
+                    n = 2 * nh + nl
+                    grp = new_grp()
+                    copy_on(
+                        nl,
+                        grp[:].rearrange("p (w j) -> p w j", j=4),
+                        raw[:, :, 512 * nl : 512 * (nl + 1)].rearrange("p j w -> p w j"),
+                    )
+                    nc.vector.quantize_mx(
+                        out=w1c[:, g, 512 * n : 512 * (n + 1)].bitcast(FP8X4),
+                        scales=w1s[4 * g : P, 512 * n : 512 * (n + 1)],
+                        in_=grp[:],
+                    )
+
+        sums = {}
+        fifths = {}
+        hidden = {}
+        codes = {}
+
+        def e_sum(k):
+            q, g = divmod(k, 4)
+            tok0 = NODES * (q // 2)
+            s = work.tile([P, 4, 512], F32, name="s", tag="s", bufs=2)
+            for t in range(4):
+                gt = 4 * g + t
+                for ii in range(16):
+                    tok = tok0 + 16 * (q % 2) + ii
+                    nc.scalar.activation(
+                        out=s[:, t, NODES * ii : NODES * (ii + 1)],
+                        in_=v_sb[:, gt, tok0 : tok0 + NODES],
+                        func=ACT.Identity,
+                        bias=u_sb[:, gt, tok : tok + 1],
+                        scale=ALPHA,
+                    )
+            tq = work.tile([P, 512, 4], F32, name="tq", tag="tq", bufs=2)
+            nc.scalar.activation(out=tq[:], in_=s[:].rearrange("p t c -> p c t"), func=ACT.Relu, scale=4.0)
+            sums[k] = s
+            fifths[k] = tq
+
+        def e_max(k):
+            e = work.tile([P, 512, 4], BF16, name="e", tag="e", bufs=1, align_bytes=64)
+            nc.gpsimd.tensor_tensor(
+                out=e[:], in0=sums[k][:].rearrange("p t c -> p c t"), in1=fifths[k][:], op=ALU.add
+            )
+            hidden[k] = e
+
+        def e_quant(k):
+            q, g = divmod(k, 4)
+            if g == 0:
+                ec = work.tile([P, 2048], U32, name="ec", tag="ec", bufs=2, align_bytes=64)
+                es = work.tile([P, 2048], U8, name="es", tag="es", bufs=2, align_bytes=64)
+                codes[q] = (ec, es)
+            ec, es = codes[q]
+            nc.vector.quantize_mx(
+                out=ec[:, 512 * g : 512 * (g + 1)].bitcast(FP8X4),
+                scales=es[:, 512 * g : 512 * (g + 1)],
+                in_=hidden[k][:].rearrange("p c t -> p (c t)"),
+            )
+
+        def passes(c):
+            q, nh = divmod(c, 4)
+            ec, es = codes[q]
+            banks = []
+            for mi in range(4):
+                for nl in range(2):
+                    n = 2 * nh + nl
+                    acc = psum.tile([P, 512], F32, name="acc", tag="ps")
+                    for g in range(4):
+                        m0 = 512 * g + P * mi
+                        nc.tensor.matmul_mx(
+                            out=acc[:],
+                            lhsT=ec[:, m0 : m0 + P].bitcast(FP8X4),
+                            lhsT_scale=es[:, m0 : m0 + P],
+                            rhs=w1c[:, g, 512 * n : 512 * (n + 1)].bitcast(FP8X4),
+                            rhs_scale=w1s[4 * g : P, 512 * n : 512 * (n + 1)],
+                            start=(g == 0),
+                            stop=(g == 3),
+                        )
+                    banks.append(acc)
+            return banks
+
+        def add_bias(c, banks, mi, o):
+            nh = c % 4
+            for nl in range(2):
+                n = 2 * nh + nl
+                nc.vector.tensor_tensor(
+                    out=o[:, 512 * nl : 512 * (nl + 1)],
+                    in0=banks[2 * mi + nl][:],
+                    in1=b1t[:, 512 * n : 512 * (n + 1)],
+                    op=ALU.add,
+                )
+
+        def lrelu_store(c, mi, o):
+            q, nh = divmod(c, 4)
+            nc.vector.scalar_tensor_tensor(out=o[:], in0=o[:], scalar=ALPHA, in1=o[:], op0=ALU.mult, op1=ALU.max)
+            r0 = 512 * q + P * mi
+            nc.sync.dma_start(out=out2[r0 : r0 + P, 1024 * nh : 1024 * (nh + 1)], in_=o[:])
+
+        def new_o():
+            o = work.tile([P, 1024], F32, name="o", tag="o", bufs=6)
+            return o
+
+        w1_quarter(0)
+        for k in range(4):
+            e_sum(k)
+            e_max(k)
+            e_quant(k)
+        w1_quarter(1)
+        e_sum(4)
+        e_max(4)
+        e_quant(4)
+        e_sum(5)
+        w1_quarter(2)
+        w1_quarter(3)
+        nc.sync.dma_start(out=b1t[:], in_=fe_b1.partition_broadcast(P))
+
+        with tc.manual_schedule():
+            for c in range(N_CYCLES):
+                banks = passes(c)
+                k = c + LEAD
+                if k < N_CHUNKS:
+                    e_max(k)
+                    outs = []
+                    for mi in range(4):
+                        o = new_o()
+                        add_bias(c, banks, mi, o)
+                        outs.append(o)
+                    if k + 1 < N_CHUNKS:
+                        e_sum(k + 1)
+                    for mi in range(4):
+                        lrelu_store(c, mi, outs[mi])
+                    e_quant(k)
+                else:
+                    for mi in range(4):
+                        o = new_o()
+                        add_bias(c, banks, mi, o)
+                        lrelu_store(c, mi, o)

@@ -23,6 +23,7 @@ ALPHA = 0.2
 N_CHUNKS = 64
 N_CYCLES = 64
 LEAD = 5
+CG = 320
 
 
 def tile_graph_gan_pa_l_kernel(tc, x, fe_w0, fe_b0, fe_w1, fe_b1, out):
@@ -186,6 +187,7 @@ def tile_graph_gan_pa_l_kernel(tc, x, fe_w0, fe_b0, fe_w1, fe_b1, out):
         fifths = {}
         hidden = {}
         codes = {}
+        wholes = {}
 
         def e_sum(k):
             q, g = divmod(k, 4)
@@ -202,17 +204,32 @@ def tile_graph_gan_pa_l_kernel(tc, x, fe_w0, fe_b0, fe_w1, fe_b1, out):
                         bias=u_sb[:, gt, tok : tok + 1],
                         scale=ALPHA,
                     )
-            tq = work.tile([P, 512, 4], F32, name="tq", tag="tq", bufs=2)
-            nc.scalar.activation(out=tq[:], in_=s[:].rearrange("p t c -> p c t"), func=ACT.Relu, scale=4.0)
+            tq = work.tile([P, CG, 4], F32, name="tq", tag="tq", bufs=2)
+            nc.scalar.activation(
+                out=tq[:], in_=s[:, :, 0:CG].rearrange("p t c -> p c t"), func=ACT.Relu, scale=4.0
+            )
+            ea = work.tile([P, 512 - CG, 4], BF16, name="ea", tag="ea", bufs=2)
+            nc.scalar.activation(
+                out=ea[:], in_=s[:, :, CG:512].rearrange("p t c -> p c t"), func=ACT.Copy, scale=5.0
+            )
+            eb = work.tile([P, 512 - CG, 4], BF16, name="eb", tag="eb", bufs=2)
+            nc.scalar.activation(
+                out=eb[:], in_=s[:, :, CG:512].rearrange("p t c -> p c t"), func=ACT.Copy, scale=1.0
+            )
             sums[k] = s
             fifths[k] = tq
+            wholes[k] = (ea, eb)
 
         def e_max(k):
             e = work.tile([P, 512, 4], BF16, name="e", tag="e", bufs=1, align_bytes=64)
             nc.gpsimd.tensor_tensor(
-                out=e[:], in0=sums[k][:].rearrange("p t c -> p c t"), in1=fifths[k][:], op=ALU.add
+                out=e[:, 0:CG, :], in0=sums[k][:, :, 0:CG].rearrange("p t c -> p c t"), in1=fifths[k][:], op=ALU.add
             )
             hidden[k] = e
+
+        def e_rest(k):
+            ea, eb = wholes[k]
+            nc.vector.tensor_tensor(out=hidden[k][:, CG:512, :], in0=ea[:], in1=eb[:], op=ALU.max)
 
         def e_quant(k):
             q, g = divmod(k, 4)
@@ -274,10 +291,12 @@ def tile_graph_gan_pa_l_kernel(tc, x, fe_w0, fe_b0, fe_w1, fe_b1, out):
         for k in range(4):
             e_sum(k)
             e_max(k)
+            e_rest(k)
             e_quant(k)
         w1_quarter(1)
         e_sum(4)
         e_max(4)
+        e_rest(4)
         e_quant(4)
         e_sum(5)
         w1_quarter(2)
@@ -297,6 +316,7 @@ def tile_graph_gan_pa_l_kernel(tc, x, fe_w0, fe_b0, fe_w1, fe_b1, out):
                         outs.append(o)
                     if k + 1 < N_CHUNKS:
                         e_sum(k + 1)
+                    e_rest(k)
                     for mi in range(4):
                         lrelu_store(c, mi, outs[mi])
                     e_quant(k)

@@ -39,6 +39,8 @@ def tile_graph_gan_pa_l_kernel(tc, x, fe_w0, fe_b0, fe_w1, fe_b1, out):
 
         ident = const.tile([P, P], F32, name="ident")
         make_identity(nc, ident[:])
+        identb = const.tile([P, P], BF16, name="identb")
+        make_identity(nc, identb[:])
         warm = const.tile([P, 8], F32, name="warm")
         nc.vector.memset(warm[:], 0.0)
         warm2 = const.tile([P, 8], F32, name="warm2")
@@ -61,11 +63,30 @@ def tile_graph_gan_pa_l_kernel(tc, x, fe_w0, fe_b0, fe_w1, fe_b1, out):
             grp = stream.tile([P, 2048], BF16, name="grp", tag="grp", bufs=4, align_bytes=64)
             return grp
 
-        def copy_on(which, dst, src):
+        def interleave(which, grp, dst, src, quarters):
             if which == 0:
                 nc.vector.tensor_copy(out=dst, in_=src)
-            else:
+            elif which == 1:
                 nc.scalar.copy(out=dst, in_=src)
+            else:
+                for hb in range(2):
+                    pb = psum.tile([P, 1024], BF16, name="pb", tag="ps")
+                    for i in range(2):
+                        nc.tensor.matmul(
+                            out=pb[:, 512 * i : 512 * (i + 1)],
+                            lhsT=identb[:],
+                            rhs=quarters[2 * hb + i],
+                            start=True,
+                            stop=True,
+                        )
+                    nc.scalar.copy(out=grp[:, 1024 * hb : 1024 * (hb + 1)], in_=pb[:])
+
+        def who(chunk, half):
+            if half == 1:
+                return 2
+            if chunk % 4 == 3:
+                return 1
+            return 0
 
         with tc.tile_pool(name="head", bufs=1) as head:
             xc = head.tile([P, 4 * TOK], U32, name="xc", align_bytes=64)
@@ -120,10 +141,15 @@ def tile_graph_gan_pa_l_kernel(tc, x, fe_w0, fe_b0, fe_w1, fe_b1, out):
                         for gl in range(2):
                             gf = 2 * fh + gl
                             grp = new_grp()
-                            copy_on(
-                                gl,
+                            interleave(
+                                who(8 * h + 2 * gk + fh, gl),
+                                grp,
                                 grp[:].rearrange("p (t m j) -> p t m j", t=4, j=4),
                                 raw[:, :, 512 * gl : 512 * (gl + 1)].rearrange("p j (m t) -> p t m j", t=4),
+                                [
+                                    raw[:, :, 512 * gl + t : 512 * (gl + 1) : 4].rearrange("p j m -> p m j")
+                                    for t in range(4)
+                                ],
                             )
                             nc.vector.quantize_mx(
                                 out=w0c[h][:, gk, 512 * gf : 512 * (gf + 1)].bitcast(FP8X4),
@@ -172,10 +198,15 @@ def tile_graph_gan_pa_l_kernel(tc, x, fe_w0, fe_b0, fe_w1, fe_b1, out):
                 for nl in range(2):
                     n = 2 * nh + nl
                     grp = new_grp()
-                    copy_on(
-                        nl,
+                    interleave(
+                        who(4 * nh + g, nl),
+                        grp,
                         grp[:].rearrange("p (w j) -> p w j", j=4),
                         raw[:, :, 512 * nl : 512 * (nl + 1)].rearrange("p j w -> p w j"),
+                        [
+                            raw[:, :, 512 * nl + P * i : 512 * nl + P * (i + 1)].rearrange("p j w -> p w j")
+                            for i in range(4)
+                        ],
                     )
                     nc.vector.quantize_mx(
                         out=w1c[:, g, 512 * n : 512 * (n + 1)].bitcast(FP8X4),
@@ -189,7 +220,7 @@ def tile_graph_gan_pa_l_kernel(tc, x, fe_w0, fe_b0, fe_w1, fe_b1, out):
         codes = {}
         wholes = {}
 
-        def e_sum(k):
+        def e_sum(k, shared=True):
             q, g = divmod(k, 4)
             tok0 = NODES * (q // 2)
             s = work.tile([P, 4, 512], F32, name="s", tag="s", bufs=2)
@@ -204,6 +235,9 @@ def tile_graph_gan_pa_l_kernel(tc, x, fe_w0, fe_b0, fe_w1, fe_b1, out):
                         bias=u_sb[:, gt, tok : tok + 1],
                         scale=ALPHA,
                     )
+            sums[k] = s
+            if not shared:
+                return
             tq = work.tile([P, CG, 4], F32, name="tq", tag="tq", bufs=2)
             nc.scalar.activation(
                 out=tq[:], in_=s[:, :, 0:CG].rearrange("p t c -> p c t"), func=ACT.Relu, scale=4.0
@@ -225,6 +259,12 @@ def tile_graph_gan_pa_l_kernel(tc, x, fe_w0, fe_b0, fe_w1, fe_b1, out):
             nc.gpsimd.tensor_tensor(
                 out=e[:, 0:CG, :], in0=sums[k][:, :, 0:CG].rearrange("p t c -> p c t"), in1=fifths[k][:], op=ALU.add
             )
+            hidden[k] = e
+
+        def e_whole(k):
+            e = work.tile([P, 512, 4], BF16, name="e", tag="e", bufs=1, align_bytes=64)
+            sv = sums[k][:].rearrange("p t c -> p c t")
+            nc.vector.scalar_tensor_tensor(out=e[:], in0=sv, scalar=5.0, in1=sv, op0=ALU.mult, op1=ALU.max)
             hidden[k] = e
 
         def e_rest(k):
@@ -288,20 +328,18 @@ def tile_graph_gan_pa_l_kernel(tc, x, fe_w0, fe_b0, fe_w1, fe_b1, out):
             return o
 
         w1_quarter(0)
+        nc.sync.dma_start(out=b1t[:], in_=fe_b1.partition_broadcast(P))
+        e_sum(0, shared=False)
         for k in range(4):
-            e_sum(k)
-            e_max(k)
-            e_rest(k)
+            e_sum(k + 1, shared=False)
+            e_whole(k)
             e_quant(k)
         w1_quarter(1)
-        e_sum(4)
-        e_max(4)
-        e_rest(4)
-        e_quant(4)
+        e_whole(4)
         e_sum(5)
+        e_quant(4)
         w1_quarter(2)
         w1_quarter(3)
-        nc.sync.dma_start(out=b1t[:], in_=fe_b1.partition_broadcast(P))
 
         with tc.manual_schedule():
             for c in range(N_CYCLES):

@@ -39,8 +39,6 @@ def tile_graph_gan_pa_l_kernel(tc, x, fe_w0, fe_b0, fe_w1, fe_b1, out):
 
         ident = const.tile([P, P], F32, name="ident")
         make_identity(nc, ident[:])
-        identb = const.tile([P, P], BF16, name="identb")
-        make_identity(nc, identb[:])
         warm = const.tile([P, 8], F32, name="warm")
         nc.vector.memset(warm[:], 0.0)
         warm2 = const.tile([P, 8], F32, name="warm2")
@@ -63,30 +61,11 @@ def tile_graph_gan_pa_l_kernel(tc, x, fe_w0, fe_b0, fe_w1, fe_b1, out):
             grp = stream.tile([P, 2048], BF16, name="grp", tag="grp", bufs=4, align_bytes=64)
             return grp
 
-        def interleave(which, grp, dst, src, quarters):
+        def copy_on(which, dst, src):
             if which == 0:
                 nc.vector.tensor_copy(out=dst, in_=src)
-            elif which == 1:
-                nc.scalar.copy(out=dst, in_=src)
             else:
-                for hb in range(2):
-                    pb = psum.tile([P, 1024], BF16, name="pb", tag="ps")
-                    for i in range(2):
-                        nc.tensor.matmul(
-                            out=pb[:, 512 * i : 512 * (i + 1)],
-                            lhsT=identb[:],
-                            rhs=quarters[2 * hb + i],
-                            start=True,
-                            stop=True,
-                        )
-                    nc.scalar.copy(out=grp[:, 1024 * hb : 1024 * (hb + 1)], in_=pb[:])
-
-        def who(chunk, half):
-            if half == 1:
-                return 2
-            if chunk % 4 == 3:
-                return 1
-            return 0
+                nc.scalar.copy(out=dst, in_=src)
 
         with tc.tile_pool(name="head", bufs=1) as head:
             xc = head.tile([P, 4 * TOK], U32, name="xc", align_bytes=64)
@@ -141,15 +120,10 @@ def tile_graph_gan_pa_l_kernel(tc, x, fe_w0, fe_b0, fe_w1, fe_b1, out):
                         for gl in range(2):
                             gf = 2 * fh + gl
                             grp = new_grp()
-                            interleave(
-                                who(8 * h + 2 * gk + fh, gl),
-                                grp,
+                            copy_on(
+                                gl,
                                 grp[:].rearrange("p (t m j) -> p t m j", t=4, j=4),
                                 raw[:, :, 512 * gl : 512 * (gl + 1)].rearrange("p j (m t) -> p t m j", t=4),
-                                [
-                                    raw[:, :, 512 * gl + t : 512 * (gl + 1) : 4].rearrange("p j m -> p m j")
-                                    for t in range(4)
-                                ],
                             )
                             nc.vector.quantize_mx(
                                 out=w0c[h][:, gk, 512 * gf : 512 * (gf + 1)].bitcast(FP8X4),
@@ -198,15 +172,10 @@ def tile_graph_gan_pa_l_kernel(tc, x, fe_w0, fe_b0, fe_w1, fe_b1, out):
                 for nl in range(2):
                     n = 2 * nh + nl
                     grp = new_grp()
-                    interleave(
-                        who(4 * nh + g, nl),
-                        grp,
+                    copy_on(
+                        nl,
                         grp[:].rearrange("p (w j) -> p w j", j=4),
                         raw[:, :, 512 * nl : 512 * (nl + 1)].rearrange("p j w -> p w j"),
-                        [
-                            raw[:, :, 512 * nl + P * i : 512 * nl + P * (i + 1)].rearrange("p j w -> p w j")
-                            for i in range(4)
-                        ],
                     )
                     nc.vector.quantize_mx(
                         out=w1c[:, g, 512 * n : 512 * (n + 1)].bitcast(FP8X4),
@@ -220,7 +189,7 @@ def tile_graph_gan_pa_l_kernel(tc, x, fe_w0, fe_b0, fe_w1, fe_b1, out):
         codes = {}
         wholes = {}
 
-        def e_sum(k, shared=True):
+        def e_sum(k):
             q, g = divmod(k, 4)
             tok0 = NODES * (q // 2)
             s = work.tile([P, 4, 512], F32, name="s", tag="s", bufs=2)
@@ -235,9 +204,6 @@ def tile_graph_gan_pa_l_kernel(tc, x, fe_w0, fe_b0, fe_w1, fe_b1, out):
                         bias=u_sb[:, gt, tok : tok + 1],
                         scale=ALPHA,
                     )
-            sums[k] = s
-            if not shared:
-                return
             tq = work.tile([P, CG, 4], F32, name="tq", tag="tq", bufs=2)
             nc.scalar.activation(
                 out=tq[:], in_=s[:, :, 0:CG].rearrange("p t c -> p c t"), func=ACT.Relu, scale=4.0
@@ -259,12 +225,6 @@ def tile_graph_gan_pa_l_kernel(tc, x, fe_w0, fe_b0, fe_w1, fe_b1, out):
             nc.gpsimd.tensor_tensor(
                 out=e[:, 0:CG, :], in0=sums[k][:, :, 0:CG].rearrange("p t c -> p c t"), in1=fifths[k][:], op=ALU.add
             )
-            hidden[k] = e
-
-        def e_whole(k):
-            e = work.tile([P, 512, 4], BF16, name="e", tag="e", bufs=1, align_bytes=64)
-            sv = sums[k][:].rearrange("p t c -> p c t")
-            nc.vector.scalar_tensor_tensor(out=e[:], in0=sv, scalar=5.0, in1=sv, op0=ALU.mult, op1=ALU.max)
             hidden[k] = e
 
         def e_rest(k):
@@ -311,35 +271,47 @@ def tile_graph_gan_pa_l_kernel(tc, x, fe_w0, fe_b0, fe_w1, fe_b1, out):
             for nl in range(2):
                 n = 2 * nh + nl
                 nc.vector.tensor_tensor(
-                    out=o[:, 512 * nl : 512 * (nl + 1)],
+                    out=o[:, mi % 2, 512 * nl : 512 * (nl + 1)],
                     in0=banks[2 * mi + nl][:],
                     in1=b1t[:, 512 * n : 512 * (n + 1)],
                     op=ALU.add,
                 )
 
-        def lrelu_store(c, mi, o):
+        def lrelu_store(c, mh, o):
             q, nh = divmod(c, 4)
-            nc.vector.scalar_tensor_tensor(out=o[:], in0=o[:], scalar=ALPHA, in1=o[:], op0=ALU.mult, op1=ALU.max)
+            ov = o[:].rearrange("p a n -> p (a n)")
+            nc.vector.scalar_tensor_tensor(out=ov, in0=ov, scalar=ALPHA, in1=ov, op0=ALU.mult, op1=ALU.max)
+            r0 = 512 * q + 2 * P * mh
+            nc.sync.dma_start(
+                out=out2[r0 : r0 + 2 * P, 1024 * nh : 1024 * (nh + 1)].rearrange("(a p) n -> p a n", a=2), in_=o[:]
+            )
+
+        def lrelu_store_half(c, mi, o):
+            q, nh = divmod(c, 4)
+            ov = o[:, mi % 2, :]
+            nc.vector.scalar_tensor_tensor(out=ov, in0=ov, scalar=ALPHA, in1=ov, op0=ALU.mult, op1=ALU.max)
             r0 = 512 * q + P * mi
-            nc.sync.dma_start(out=out2[r0 : r0 + P, 1024 * nh : 1024 * (nh + 1)], in_=o[:])
+            nc.sync.dma_start(out=out2[r0 : r0 + P, 1024 * nh : 1024 * (nh + 1)], in_=ov)
 
         def new_o():
-            o = work.tile([P, 1024], F32, name="o", tag="o", bufs=6)
+            o = work.tile([P, 2, 1024], F32, name="o", tag="o", bufs=4)
             return o
 
         w1_quarter(0)
-        nc.sync.dma_start(out=b1t[:], in_=fe_b1.partition_broadcast(P))
-        e_sum(0, shared=False)
         for k in range(4):
-            e_sum(k + 1, shared=False)
-            e_whole(k)
+            e_sum(k)
+            e_max(k)
+            e_rest(k)
             e_quant(k)
         w1_quarter(1)
-        e_whole(4)
-        e_sum(5)
+        e_sum(4)
+        e_max(4)
+        e_rest(4)
         e_quant(4)
+        e_sum(5)
         w1_quarter(2)
         w1_quarter(3)
+        nc.sync.dma_start(out=b1t[:], in_=fe_b1.partition_broadcast(P))
 
         with tc.manual_schedule():
             for c in range(N_CYCLES):
@@ -348,18 +320,20 @@ def tile_graph_gan_pa_l_kernel(tc, x, fe_w0, fe_b0, fe_w1, fe_b1, out):
                 if k < N_CHUNKS:
                     e_max(k)
                     outs = []
-                    for mi in range(4):
+                    for mh in range(2):
                         o = new_o()
-                        add_bias(c, banks, mi, o)
+                        add_bias(c, banks, 2 * mh, o)
+                        add_bias(c, banks, 2 * mh + 1, o)
                         outs.append(o)
                     if k + 1 < N_CHUNKS:
                         e_sum(k + 1)
                     e_rest(k)
-                    for mi in range(4):
-                        lrelu_store(c, mi, outs[mi])
+                    lrelu_store(c, 0, outs[0])
                     e_quant(k)
+                    lrelu_store(c, 1, outs[1])
                 else:
-                    for mi in range(4):
+                    for mh in range(2):
                         o = new_o()
-                        add_bias(c, banks, mi, o)
-                        lrelu_store(c, mi, o)
+                        for mi in (2 * mh, 2 * mh + 1):
+                            add_bias(c, banks, mi, o)
+                            lrelu_store_half(c, mi, o)

@@ -23,7 +23,8 @@ ALPHA = 0.2
 N_CHUNKS = 64
 N_CYCLES = 64
 LEAD = 5
-CG = 320
+CG = 64
+G_LAST = 57
 
 
 def tile_graph_gan_pa_l_kernel(tc, x, fe_w0, fe_b0, fe_w1, fe_b1, out):
@@ -58,7 +59,7 @@ def tile_graph_gan_pa_l_kernel(tc, x, fe_w0, fe_b0, fe_w1, fe_b1, out):
             return raw
 
         def new_grp():
-            grp = stream.tile([P, 2048], BF16, name="grp", tag="grp", bufs=4, align_bytes=64)
+            grp = stream.tile([P, 2048], BF16, name="grp", tag="grp", bufs=3, align_bytes=64)
             return grp
 
         def copy_on(which, dst, src):
@@ -293,6 +294,17 @@ def tile_graph_gan_pa_l_kernel(tc, x, fe_w0, fe_b0, fe_w1, fe_b1, out):
             r0 = 512 * q + P * mi
             nc.sync.dma_start(out=out2[r0 : r0 + P, 1024 * nh : 1024 * (nh + 1)], in_=ov)
 
+        def s_relu(o):
+            rg = work.tile([P, 1024], F32, name="rg", tag="rg", bufs=1)
+            nc.scalar.activation(out=rg[:], in_=o[:, 1, :], func=ACT.Relu, scale=ALPHA - 1.0)
+            return rg
+
+        def g_finish(c, o, rg):
+            q, nh = divmod(c, 4)
+            nc.gpsimd.tensor_tensor(out=o[:, 1, :], in0=o[:, 1, :], in1=rg[:], op=ALU.add)
+            r0 = 512 * q + 3 * P
+            nc.sync.dma_start(out=out2[r0 : r0 + P, 1024 * nh : 1024 * (nh + 1)], in_=o[:, 1, :])
+
         def new_o():
             o = work.tile([P, 2, 1024], F32, name="o", tag="o", bufs=4)
             return o
@@ -313,12 +325,16 @@ def tile_graph_gan_pa_l_kernel(tc, x, fe_w0, fe_b0, fe_w1, fe_b1, out):
         w1_quarter(3)
         nc.sync.dma_start(out=b1t[:], in_=fe_b1.partition_broadcast(P))
 
+        pending = []
         with tc.manual_schedule():
             for c in range(N_CYCLES):
                 banks = passes(c)
                 k = c + LEAD
                 if k < N_CHUNKS:
                     e_max(k)
+                    if len(pending) > 0:
+                        g_finish(c - 1, pending[0], pending[1])
+                        pending = []
                     outs = []
                     for mh in range(2):
                         o = new_o()
@@ -327,10 +343,15 @@ def tile_graph_gan_pa_l_kernel(tc, x, fe_w0, fe_b0, fe_w1, fe_b1, out):
                         outs.append(o)
                     if k + 1 < N_CHUNKS:
                         e_sum(k + 1)
+                    if c <= G_LAST:
+                        pending = [outs[1], s_relu(outs[1])]
                     e_rest(k)
-                    lrelu_store(c, 0, outs[0])
+                    if c <= G_LAST:
+                        lrelu_store_half(c, 2, outs[1])
+                    else:
+                        lrelu_store(c, 1, outs[1])
                     e_quant(k)
-                    lrelu_store(c, 1, outs[1])
+                    lrelu_store(c, 0, outs[0])
                 else:
                     for mh in range(2):
                         o = new_o()

from contextlib import ExitStack

import concourse.mybir as mybir
from concourse.masks import make_identity

FLOPS = 2 * 256 * 2048 * 4096 + 2 * 8192 * 2048 * 4096

F32 = mybir.dt.float32
BF16 = mybir.dt.bfloat16
U32 = mybir.dt.uint32
U8 = mybir.dt.uint8
FP8X4 = mybir.dt.float8_e4m3fn_x4
ACT = mybir.ActivationFunctionType
ALU = mybir.AluOpType

P = 128
NODES = 32
TOK = 256
D = 2048
F1 = 2048
F2 = 4096
ALPHA = 0.2
N_CHUNKS = 64
N_CYCLES = 64
LEAD = 5
CG = 64
G_LAST = 57


def tile_graph_gan_pa_l_kernel(tc, x, fe_w0, fe_b0, fe_w1, fe_b1, out):
    nc = tc.nc
    x2 = x.rearrange("b n d -> (b n) d")
    out2 = out.rearrange("b i j c -> (b i j) c")

    with ExitStack() as ctx:
        const = ctx.enter_context(tc.tile_pool(name="const", bufs=1))
        keep = ctx.enter_context(tc.tile_pool(name="keep", bufs=1))
        stream = ctx.enter_context(tc.tile_pool(name="stream", bufs=3))
        psum = ctx.enter_context(tc.psum_pool(name="psum", bufs=8))

        ident = const.tile([P, P], F32, name="ident")
        make_identity(nc, ident[:])
        warm = const.tile([P, 8], F32, name="warm")
        nc.vector.memset(warm[:], 0.0)
        warm2 = const.tile([P, 8], F32, name="warm2")
        nc.scalar.activation(out=warm2[:], in_=warm[:], func=ACT.Identity)
        b0raw = const.tile([P, 4, 4], BF16, name="b0raw")
        b0f = const.tile([P, 16], F32, name="b0f")
        b1t = const.tile([P, F2], BF16, name="b1t")

        w1c = keep.tile([P, 4, F2], U32, name="w1c", align_bytes=64)
        w1s = keep.tile([P, F2], U8, name="w1s", align_bytes=64)
        u_sb = keep.tile([P, 16, TOK], F32, name="u_sb")
        v_sb = keep.tile([P, 16, TOK], F32, name="v_sb")

        def load_chunk(rows):
            raw = stream.tile([P, 4, 1024], BF16, name="raw", tag="raw", bufs=3)
            nc.sync.dma_start(out=raw[:], in_=rows.rearrange("(p j) f -> p j f", j=4))
            return raw

        def new_grp():
            grp = stream.tile([P, 2048], BF16, name="grp", tag="grp", bufs=3, align_bytes=64)
            return grp

        def copy_on(which, dst, src):
            if which == 0:
                nc.vector.tensor_copy(out=dst, in_=src)
            else:
                nc.scalar.copy(out=dst, in_=src)

        with tc.tile_pool(name="head", bufs=1) as head:
            xc = head.tile([P, 4 * TOK], U32, name="xc", align_bytes=64)
            xs = head.tile([P, 4 * TOK], U8, name="xs", align_bytes=64)
            w0c = []
            w0s = []
            for h in range(2):
                w0c_h = head.tile([P, 4, F1], U32, name="w0c%d" % h, align_bytes=64)
                w0s_h = head.tile([P, F1], U8, name="w0s%d" % h, align_bytes=64)
                w0c.append(w0c_h)
                w0s.append(w0s_h)

            xraw = []
            for tt in range(2):
                xr = new_grp()
                nc.sync.dma_start(out=xr[:], in_=x2[P * tt : P * (tt + 1), :])
                xraw.append(xr)
            nc.sync.dma_start(out=b0raw[:], in_=fe_b0.rearrange("(g p t) -> p g t", g=4, t=4))
            nc.vector.tensor_copy(out=b0f[:], in_=b0raw[:].rearrange("p g t -> p (g t)"))

            for gh in range(2):
                xg = new_grp()
                for gl in range(2):
                    g = 2 * gh + gl
                    pt = psum.tile([P, 512], F32, name="pt", tag="ps")
                    for tt in range(2):
                        words = xraw[tt][:].bitcast(F32)
                        for u in range(2):
                            col = (2 * tt + u) * P
                            nc.tensor.transpose(
                                pt[:, col : col + P],
                                words[:, 256 * g + u : 256 * (g + 1) : 2],
                                ident[:],
                            )
                    nc.vector.tensor_copy(
                        out=xg[:, 1024 * gl : 1024 * (gl + 1)]
                        .bitcast(F32)
                        .rearrange("p (tt r u) -> p tt r u", tt=2, u=2),
                        in_=pt[:].rearrange("p (tt u r) -> p tt r u", tt=2, u=2),
                    )
                nc.vector.quantize_mx(
                    out=xc[:, 512 * gh : 512 * (gh + 1)].bitcast(FP8X4),
                    scales=xs[:, 512 * gh : 512 * (gh + 1)],
                    in_=xg[:],
                )

            for h in range(2):
                for gk in range(4):
                    for fh in range(2):
                        r0 = 2048 * h + 512 * gk
                        raw = load_chunk(fe_w0[r0 : r0 + 512, 1024 * fh : 1024 * (fh + 1)])
                        for gl in range(2):
                            gf = 2 * fh + gl
                            grp = new_grp()
                            copy_on(
                                gl,
                                grp[:].rearrange("p (t m j) -> p t m j", t=4, j=4),
                                raw[:, :, 512 * gl : 512 * (gl + 1)].rearrange("p j (m t) -> p t m j", t=4),
                            )
                            nc.vector.quantize_mx(
                                out=w0c[h][:, gk, 512 * gf : 512 * (gf + 1)].bitcast(FP8X4),
                                scales=w0s[h][4 * gk : P, 512 * gf : 512 * (gf + 1)],
                                in_=grp[:],
                            )
                for gf in range(4):
                    for th in range(2):
                        ps1 = psum.tile([P, 512], F32, name="ps1", tag="ps")
                        for tl in range(2):
                            t = 2 * th + tl
                            c0 = 512 * gf + P * t
                            for gk in range(4):
                                nc.tensor.matmul_mx(
                                    out=ps1[:, TOK * tl : TOK * (tl + 1)],
                                    lhsT=w0c[h][:, gk, c0 : c0 + P].bitcast(FP8X4),
                                    lhsT_scale=w0s[h][4 * gk : P, c0 : c0 + P],
                                    rhs=xc[:, TOK * gk : TOK * (gk + 1)].bitcast(FP8X4),
                                    rhs_scale=xs[:, TOK * gk : TOK * (gk + 1)],
                                    start=(gk == 0),
                                    stop=(gk == 3),
                                )
                        gt = 4 * gf + 2 * th
                        if h == 0:
                            dst = u_sb[:, gt : gt + 2, :].rearrange("p a r -> p (a r)")
                            if th == 0:
                                nc.vector.tensor_scalar_mul(out=dst, in0=ps1[:], scalar1=ALPHA)
                            else:
                                nc.scalar.activation(out=dst, in_=ps1[:], func=ACT.Copy, scale=ALPHA)
                        else:
                            for tl in range(2):
                                src = ps1[:, TOK * tl : TOK * (tl + 1)]
                                bias = b0f[:, gt + tl : gt + tl + 1]
                                if th == 0:
                                    nc.vector.tensor_scalar_add(out=v_sb[:, gt + tl, :], in0=src, scalar1=bias)
                                else:
                                    nc.scalar.activation(
                                        out=v_sb[:, gt + tl, :], in_=src, func=ACT.Identity, bias=bias, scale=1.0
                                    )

        work = ctx.enter_context(tc.tile_pool(name="work", bufs=2))

        def w1_quarter(nh):
            for g in range(4):
                raw = load_chunk(fe_w1[512 * g : 512 * (g + 1), 1024 * nh : 1024 * (nh + 1)])
                for nl in range(2):
                    n = 2 * nh + nl
                    grp = new_grp()
                    copy_on(
                        nl,
                        grp[:].rearrange("p (w j) -> p w j", j=4),
                        raw[:, :, 512 * nl : 512 * (nl + 1)].rearrange("p j w -> p w j"),
                    )
                    nc.vector.quantize_mx(
                        out=w1c[:, g, 512 * n : 512 * (n + 1)].bitcast(FP8X4),
                        scales=w1s[4 * g : P, 512 * n : 512 * (n + 1)],
                        in_=grp[:],
                    )

        sums = {}
        fifths = {}
        hidden = {}
        codes = {}
        wholes = {}

        def e_sum(k):
            q, g = divmod(k, 4)
            tok0 = NODES * (q // 2)
            s = work.tile([P, 4, 512], F32, name="s", tag="s", bufs=2)
            for t in range(4):
                gt = 4 * g + t
                for ii in range(16):
                    tok = tok0 + 16 * (q % 2) + ii
                    nc.scalar.activation(
                        out=s[:, t, NODES * ii : NODES * (ii + 1)],
                        in_=v_sb[:, gt, tok0 : tok0 + NODES],
                        func=ACT.Identity,
                        bias=u_sb[:, gt, tok : tok + 1],
                        scale=ALPHA,
                    )
            tq = work.tile([P, CG, 4], F32, name="tq", tag="tq", bufs=2)
            nc.scalar.activation(
                out=tq[:], in_=s[:, :, 0:CG].rearrange("p t c -> p c t"), func=ACT.Relu, scale=4.0
            )
            ea = work.tile([P, 512 - CG, 4], BF16, name="ea", tag="ea", bufs=2)
            nc.scalar.activation(
                out=ea[:], in_=s[:, :, CG:512].rearrange("p t c -> p c t"), func=ACT.Copy, scale=5.0
            )
            eb = work.tile([P, 512 - CG, 4], BF16, name="eb", tag="eb", bufs=2)
            nc.scalar.activation(
                out=eb[:], in_=s[:, :, CG:512].rearrange("p t c -> p c t"), func=ACT.Copy, scale=1.0
            )
            sums[k] = s
            fifths[k] = tq
            wholes[k] = (ea, eb)

        def e_max(k):
            e = work.tile([P, 512, 4], BF16, name="e", tag="e", bufs=1, align_bytes=64)
            nc.gpsimd.tensor_tensor(
                out=e[:, 0:CG, :], in0=sums[k][:, :, 0:CG].rearrange("p t c -> p c t"), in1=fifths[k][:], op=ALU.add
            )
            hidden[k] = e

        def e_rest(k):
            ea, eb = wholes[k]
            nc.vector.tensor_tensor(out=hidden[k][:, CG:512, :], in0=ea[:], in1=eb[:], op=ALU.max)

        def e_quant(k):
            q, g = divmod(k, 4)
            if g == 0:
                ec = work.tile([P, 2048], U32, name="ec", tag="ec", bufs=2, align_bytes=64)
                es = work.tile([P, 2048], U8, name="es", tag="es", bufs=2, align_bytes=64)
                codes[q] = (ec, es)
            ec, es = codes[q]
            nc.vector.quantize_mx(
                out=ec[:, 512 * g : 512 * (g + 1)].bitcast(FP8X4),
                scales=es[:, 512 * g : 512 * (g + 1)],
                in_=hidden[k][:].rearrange("p c t -> p (c t)"),
            )

        def passes(c):
            q, nh = divmod(c, 4)
            ec, es = codes[q]
            banks = []
            for mi in range(4):
                for nl in range(2):
                    n = 2 * nh + nl
                    acc = psum.tile([P, 512], F32, name="acc", tag="ps")
                    for g in range(4):
                        m0 = 512 * g + P * mi
                        nc.tensor.matmul_mx(
                            out=acc[:],
                            lhsT=ec[:, m0 : m0 + P].bitcast(FP8X4),
                            lhsT_scale=es[:, m0 : m0 + P],
                            rhs=w1c[:, g, 512 * n : 512 * (n + 1)].bitcast(FP8X4),
                            rhs_scale=w1s[4 * g : P, 512 * n : 512 * (n + 1)],
                            start=(g == 0),
                            stop=(g == 3),
                        )
                    banks.append(acc)
            return banks

        def add_bias(c, banks, mi, o):
            nh = c % 4
            for nl in range(2):
                n = 2 * nh + nl
                nc.vector.tensor_tensor(
                    out=o[:, mi % 2, 512 * nl : 512 * (nl + 1)],
                    in0=banks[2 * mi + nl][:],
                    in1=b1t[:, 512 * n : 512 * (n + 1)],
                    op=ALU.add,
                )

        def lrelu_store(c, mh, o):
            q, nh = divmod(c, 4)
            ov = o[:].rearrange("p a n -> p (a n)")
            nc.vector.scalar_tensor_tensor(out=ov, in0=ov, scalar=ALPHA, in1=ov, op0=ALU.mult, op1=ALU.max)
            r0 = 512 * q + 2 * P * mh
            nc.sync.dma_start(
                out=out2[r0 : r0 + 2 * P, 1024 * nh : 1024 * (nh + 1)].rearrange("(a p) n -> p a n", a=2), in_=o[:]
            )

        def lrelu_store_half(c, mi, o):
            q, nh = divmod(c, 4)
            ov = o[:, mi % 2, :]
            nc.vector.scalar_tensor_tensor(out=ov, in0=ov, scalar=ALPHA, in1=ov, op0=ALU.mult, op1=ALU.max)
            r0 = 512 * q + P * mi
            nc.sync.dma_start(out=out2[r0 : r0 + P, 1024 * nh : 1024 * (nh + 1)], in_=ov)

        def s_relu(o):
            rg = work.tile([P, 1024], F32, name="rg", tag="rg", bufs=1)
            nc.scalar.activation(out=rg[:], in_=o[:, 1, :], func=ACT.Relu, scale=ALPHA - 1.0)
            return rg

        def g_finish(c, o, rg):
            q, nh = divmod(c, 4)
            nc.gpsimd.tensor_tensor(out=o[:, 1, :], in0=o[:, 1, :], in1=rg[:], op=ALU.add)
            r0 = 512 * q + 3 * P
            nc.sync.dma_start(out=out2[r0 : r0 + P, 1024 * nh : 1024 * (nh + 1)], in_=o[:, 1, :])

        def new_o():
            o = work.tile([P, 2, 1024], F32, name="o", tag="o", bufs=4)
            return o

        w1_quarter(0)
        for k in range(4):
            e_sum(k)
            e_max(k)
            e_rest(k)
            e_quant(k)
        w1_quarter(1)
        e_sum(4)
        e_max(4)
        e_rest(4)
        e_quant(4)
        e_sum(5)
        w1_quarter(2)
        w1_quarter(3)
        nc.sync.dma_start(out=b1t[:], in_=fe_b1.partition_broadcast(P))

        pending = []
        with tc.manual_schedule():
            for c in range(N_CYCLES):
                banks = passes(c)
                k = c + LEAD
                if k < N_CHUNKS:
                    e_max(k)
                    if len(pending) > 0:
                        g_finish(c - 1, pending[0], pending[1])
                        pending = []
                    outs = []
                    for mh in range(2):
                        o = new_o()
                        add_bias(c, banks, 2 * mh, o)
                        add_bias(c, banks, 2 * mh + 1, o)
                        outs.append(o)
                    if k + 1 < N_CHUNKS:
                        e_sum(k + 1)
                    if c <= G_LAST:
                        pending = [outs[1], s_relu(outs[1])]
                    e_rest(k)
                    if c <= G_LAST:
                        lrelu_store_half(c, 2, outs[1])
                    else:
                        lrelu_store(c, 1, outs[1])
                    e_quant(k)
                    lrelu_store(c, 0, outs[0])
                else:
                    for mh in range(2):
                        o = new_o()
                        for mi in (2 * mh, 2 * mh + 1):
                            add_bias(c, banks, mi, o)
                            lrelu_store_half(c, mi, o)
